import numpy as np
import ml_dtypes


def mxq(x, axis, fmt="e4m3"):
    dtype, down = {"e4m3": (ml_dtypes.float8_e4m3fn, 7), "e5m2": (ml_dtypes.float8_e5m2, 14)}[fmt]
    v = np.moveaxis(np.asarray(x, np.float32).astype(ml_dtypes.bfloat16).astype(np.float64), axis, -1)
    blocks = v.reshape(v.shape[:-1] + (-1, 32))
    amax = np.abs(blocks).max(-1, keepdims=True)
    byte = np.maximum(np.where(amax > 0, np.frexp(amax)[1] - 1 + 127, 0) - down, 1)
    scale = np.exp2(byte - 127.0)
    codes = (blocks / scale).astype(np.float32).astype(dtype).astype(np.float64)
    return np.moveaxis((codes * scale).reshape(v.shape), -1, axis)


WIDE = False


def mx_kscale(k):
    if not WIDE:
        return np.ones(k)
    levels = np.array([10, -10, 5, -5, 0])
    a = np.random.permutation(np.resize(levels, k // 512 * 4)).reshape(k // 512, 4)
    idx = np.arange(k)
    return np.exp2(a[idx // 512, idx % 128 // 32])


BF16 = ml_dtypes.bfloat16


def bf(x):
    return np.asarray(x, np.float32).astype(BF16)


def f64(x):
    return np.asarray(x).astype(np.float64)


B, S, D, H, DK, F = 2, 2048, 512, 4, 128, 256
HD = H * DK
EPS = 1e-6


def rmsnorm(v, g):
    return v / np.sqrt(np.mean(v * v, axis=-1, keepdims=True) + EPS) * g


def silu(v):
    return v / (1.0 + np.exp(-v))


def setup_inputs():
    s, t = mx_kscale(HD), mx_kscale(D)
    return {"x": bf(np.random.standard_normal((B, S, D))),
            "ao": bf(np.random.standard_normal((B, H, S, DK)) * 0.3 * s.reshape(H, 1, DK)),
            "wo": bf(np.random.standard_normal((HD, D)) * 1.5 / np.sqrt(HD) / s[:, None]),
            "bo": bf(np.random.standard_normal(D) * 0.1),
            "g2": bf((1.0 + 0.1 * np.random.standard_normal(D)) * t),
            "w1": bf(np.random.standard_normal((D, F)) / np.sqrt(D) / t[:, None]),
            "w3": bf(np.random.standard_normal((D, F)) / np.sqrt(D) / t[:, None])}


def reference(x, ao, wo, bo, g2, w1, w3):
    a = f64(ao).transpose(0, 2, 1, 3).reshape(B, S, HD)
    x1 = f64(x) + ((mxq(a, 2, "e4m3") @ mxq(f64(wo), 0, "e4m3")) + f64(bo))
    n = mxq(rmsnorm(x1, f64(g2)), 2, "e4m3")
    h = silu(n @ mxq(f64(w1), 0, "e4m3")) * (n @ mxq(f64(w3), 0, "e4m3"))
    return x1, h

@@ -1,0 +1,286 @@
+from contextlib import ExitStack
+
+import concourse.mybir as mybir
+from concourse.masks import make_identity
+
+BF16 = mybir.dt.bfloat16
+F32 = mybir.dt.float32
+U32 = mybir.dt.uint32
+U8 = mybir.dt.uint8
+FP8X4 = mybir.dt.float8_e4m3fn_x4
+ALU = mybir.AluOpType
+ACT = mybir.ActivationFunctionType
+
+B, S, D, H, DK, F = 2, 2048, 512, 4, 128, 256
+EPS = 1e-6
+P = 128
+PACK = 4
+T_PER_P = S // P
+QUAD = 4
+PAIR = 2
+N_QUADS = B * T_PER_P // QUAD
+N_PAIRS = B * T_PER_P // PAIR
+FLOPS = 2 * B * S * (H * DK * D + D * 2 * F)
+
+
+def tile_transformerblock_pb_t_kernel(tc, x, ao, wo, bo, g2, w1, w3, out_0, out_1):
+    nc = tc.nc
+    x_view = x.rearrange("b (p t) d -> b p t d", t=T_PER_P)
+    ao_view = ao.rearrange("b h (p t) d -> b p h t d", t=T_PER_P)
+    x1_view = out_0.rearrange("b (p t) d -> b p t d", t=T_PER_P)
+    h_view = out_1.rearrange("b (p t) f -> b p t f", t=T_PER_P)
+
+    with ExitStack() as ctx:
+        ctx.enter_context(tc.manual_schedule())
+        consts = ctx.enter_context(tc.tile_pool(name="consts", bufs=1))
+        loads = ctx.enter_context(tc.tile_pool(name="loads", bufs=N_QUADS))
+        work = ctx.enter_context(tc.tile_pool(name="work", bufs=3))
+        outs = ctx.enter_context(tc.tile_pool(name="outs", bufs=6))
+        psum = ctx.enter_context(tc.psum_pool(name="psum", bufs=2))
+
+        vecs = consts.tile([P, 2, D], BF16)
+        nc.vector.memset(vecs[:], 0.0)
+        nc.sync.dma_start(out=vecs[0:1, 0, :], in_=bo.unsqueeze(0))
+        nc.sync.dma_start(out=vecs[0:1, 1, :], in_=g2.unsqueeze(0))
+
+        wo_raw = consts.tile([P, PACK, D], BF16)
+        w1_raw = consts.tile([P, PACK, F], BF16)
+        w3_raw = consts.tile([P, PACK, F], BF16)
+        a_sb = []
+        x_sb = []
+        for q in range(N_QUADS):
+            b, t0 = q // (T_PER_P // QUAD), (q % (T_PER_P // QUAD)) * QUAD
+            a_q = loads.tile([P, H, QUAD, DK], BF16, name="a_q", tag="a_q")
+            nc.sync.dma_start(out=a_q[:], in_=ao_view[b, :, :, t0 : t0 + QUAD, :])
+            if q == 0:
+                nc.sync.dma_start(out=wo_raw[:], in_=wo.rearrange("(j p) n -> p j n", p=P))
+            x_q = loads.tile([P, QUAD, D], BF16, name="x_q", tag="x_q")
+            nc.sync.dma_start(out=x_q[:], in_=x_view[b, :, t0 : t0 + QUAD, :])
+            if q == 0:
+                nc.sync.dma_start(
+                    out=w1_raw[:].rearrange("p (u e) f -> p u (e f)", u=2),
+                    in_=w1.rearrange("(u p e) f -> p u (e f)", u=2, e=2),
+                )
+                nc.sync.dma_start(
+                    out=w3_raw[:].rearrange("p (u e) f -> p u (e f)", u=2),
+                    in_=w3.rearrange("(u p e) f -> p u (e f)", u=2, e=2),
+                )
+            a_sb.append(a_q)
+            x_sb.append(x_q)
+
+        warm = consts.tile([P, 2], F32)
+        nc.vector.memset(warm[:], 0.0)
+        nc.scalar.activation(out=warm[:, 1:2], in_=warm[:, 0:1], func=ACT.Silu)
+        ident_bf = consts.tile([P, P], BF16)
+        make_identity(nc, ident_bf[:])
+        ident_f32 = consts.tile([P, P], F32)
+        make_identity(nc, ident_f32[:])
+        ones = consts.tile([P, P], BF16)
+        nc.vector.memset(ones[:], 1.0)
+        neg_half = consts.tile([P, PAIR], F32)
+        nc.vector.memset(neg_half[:], -0.5)
+
+        bo_ps = psum.tile([P, D], F32, tag="acc1")
+        nc.tensor.matmul(out=bo_ps[:], lhsT=ones[:], rhs=vecs[:, 0, :], start=True, stop=True)
+        bo_all = consts.tile([P, D], BF16)
+        nc.scalar.copy(out=bo_all[:], in_=bo_ps[:])
+        g2_ps = psum.tile([P, D], F32, tag="g2_ps", bufs=1)
+        nc.tensor.matmul(out=g2_ps[:], lhsT=ones[:], rhs=vecs[:, 1, :], start=True, stop=True)
+
+        wo_grp = consts.tile([P, D, PACK], BF16, align_bytes=64)
+        wo_codes = consts.tile([P, D], U32, align_bytes=64)
+        wo_scales = consts.tile([P, D], U8, align_bytes=64)
+        nc.vector.tensor_copy(out=wo_grp[:], in_=wo_raw[:].rearrange("p j n -> p n j"))
+        nc.vector.quantize_mx(
+            out=wo_codes[:].bitcast(FP8X4),
+            scales=wo_scales[:],
+            in_=wo_grp[:].rearrange("p n j -> p (n j)"),
+        )
+        w13_grp = consts.tile([P, 2 * F, PACK], BF16, align_bytes=64)
+        w13_codes = consts.tile([P, 2 * F], U32, align_bytes=64)
+        w13_scales = consts.tile([P, 2 * F], U8, align_bytes=64)
+
+        def quantise_gate_weights():
+            nc.vector.tensor_copy(out=w13_grp[:, 0:F, :], in_=w1_raw[:].rearrange("p j f -> p f j"))
+            nc.vector.tensor_copy(out=w13_grp[:, F : 2 * F, :], in_=w3_raw[:].rearrange("p j f -> p f j"))
+            nc.vector.quantize_mx(
+                out=w13_codes[:].bitcast(FP8X4),
+                scales=w13_scales[:],
+                in_=w13_grp[:].rearrange("p n j -> p (n j)"),
+            )
+
+        live = {}
+
+        def transposes_a(i):
+            a_t = psum.tile([P, H, PAIR * P], BF16, tag="a_t")
+            for j in range(PAIR):
+                for h in range(H):
+                    nc.tensor.transpose(
+                        a_t[:, h, j * P : (j + 1) * P],
+                        a_sb[i // 2][:, h, (i % 2) * PAIR + j, :],
+                        ident_bf[:],
+                    )
+            live["a_t", i] = a_t
+
+        def copy_a(i):
+            a_grp = work.tile([P, PAIR * P, PACK], BF16, align_bytes=64)
+            nc.scalar.copy(out=a_grp[:], in_=live["a_t", i][:].rearrange("p h t -> p t h"))
+            live["a_grp", i] = a_grp
+
+        def bias(i):
+            xb = work.tile([P, PAIR, D], F32)
+            for j in range(PAIR):
+                nc.gpsimd.tensor_tensor(
+                    out=xb[:, j, :], in0=x_sb[i // 2][:, (i % 2) * PAIR + j, :], in1=bo_all[:], op=ALU.add
+                )
+            live["xb", i] = xb
+
+        def quantise_a(i):
+            a_codes = work.tile([P, PAIR * P], U32, align_bytes=64)
+            a_scales = work.tile([P, PAIR * P], U8, align_bytes=64)
+            nc.vector.quantize_mx(
+                out=a_codes[:].bitcast(FP8X4),
+                scales=a_scales[:],
+                in_=live["a_grp", i][:].rearrange("p t h -> p (t h)"),
+            )
+            live["a_codes", i] = a_codes
+            live["a_scales", i] = a_scales
+
+        def project(i):
+            for j in range(PAIR):
+                cols = slice(j * P, (j + 1) * P)
+                acc1 = psum.tile([P, D], F32, tag="acc1")
+                nc.tensor.matmul_mx(
+                    out=acc1[:],
+                    lhsT=live["a_codes", i][:, cols].bitcast(FP8X4),
+                    lhsT_scale=live["a_scales", i][:, cols],
+                    rhs=wo_codes[:].bitcast(FP8X4),
+                    rhs_scale=wo_scales[:],
+                    start=True,
+                    stop=True,
+                )
+                live["acc1", i, j] = acc1
+
+        def residual(i):
+            x1 = outs.tile([P, PAIR, D], F32)
+            for j in range(PAIR):
+                nc.vector.tensor_tensor(
+                    out=x1[:, j, :], in0=live["acc1", i, j][:], in1=live["xb", i][:, j, :], op=ALU.add
+                )
+            b, t0 = i // (N_PAIRS // B), (i % (N_PAIRS // B)) * PAIR
+            nc.sync.dma_start(out=x1_view[b, :, t0 : t0 + PAIR, :], in_=x1[:])
+            live["x1", i] = x1
+
+        def squares(i):
+            ssq = work.tile([P, PAIR], F32)
+            for j in range(PAIR):
+                unread = work.tile([P, D], BF16, bufs=4)
+                nc.scalar.activation(
+                    out=unread[:], in_=live["x1", i][:, j, :], func=ACT.Square, accum_out=ssq[:, j : j + 1]
+                )
+            live["ssq", i] = ssq
+
+        def mean_square(i):
+            ms = work.tile([P, PAIR], F32)
+            nc.vector.tensor_scalar(
+                out=ms[:], in0=live["ssq", i][:], scalar1=1.0 / D, scalar2=EPS, op0=ALU.mult, op1=ALU.add
+            )
+            live["ms", i] = ms
+
+        def rsqrt(i):
+            r = work.tile([P, PAIR], F32)
+            nc.gpsimd.tensor_tensor(out=r[:], in0=live["ms", i][:], in1=neg_half[:], op=ALU.pow)
+            live["r", i] = r
+
+        def normalise(i):
+            n_sb = work.tile([P, PAIR, D], BF16)
+            for j in range(PAIR):
+                nc.vector.scalar_tensor_tensor(
+                    out=n_sb[:, j, :],
+                    in0=live["x1", i][:, j, :],
+                    scalar=live["r", i][:, j : j + 1],
+                    in1=g2_ps[:],
+                    op0=ALU.mult,
+                    op1=ALU.mult,
+                )
+            live["n_sb", i] = n_sb
+
+        def transposes_n(i):
+            n_t = psum.tile([P, 2, PAIR * P], F32, tag="n_t", bufs=1)
+            for j in range(PAIR):
+                n_words = live["n_sb", i][:, j, :].bitcast(F32)
+                for u in range(2):
+                    nc.tensor.transpose(
+                        n_t[:, u, j * P : (j + 1) * P], n_words[:, u * P : (u + 1) * P], ident_f32[:]
+                    )
+            live["n_t", i] = n_t
+
+        def copy_n(i):
+            n_grp = work.tile([P, PAIR * P, 2], F32, align_bytes=64)
+            nc.scalar.copy(out=n_grp[:], in_=live["n_t", i][:].rearrange("p u t -> p t u"))
+            live["n_grp", i] = n_grp
+
+        def quantise_n(i):
+            n_codes = work.tile([P, PAIR * P], U32, align_bytes=64)
+            n_scales = work.tile([P, PAIR * P], U8, align_bytes=64)
+            nc.vector.quantize_mx(
+                out=n_codes[:].bitcast(FP8X4),
+                scales=n_scales[:],
+                in_=live["n_grp", i][:].rearrange("p t u -> p (t u)").bitcast(BF16),
+            )
+            live["n_codes", i] = n_codes
+            live["n_scales", i] = n_scales
+
+        def gate_matmuls(i):
+            for j in range(PAIR):
+                cols = slice(j * P, (j + 1) * P)
+                acc2 = psum.tile([P, 2 * F], F32, tag="acc2")
+                nc.tensor.matmul_mx(
+                    out=acc2[:],
+                    lhsT=live["n_codes", i][:, cols].bitcast(FP8X4),
+                    lhsT_scale=live["n_scales", i][:, cols],
+                    rhs=w13_codes[:].bitcast(FP8X4),
+                    rhs_scale=w13_scales[:],
+                    start=True,
+                    stop=True,
+                )
+                live["acc2", i, j] = acc2
+
+        def silu(i):
+            for j in range(PAIR):
+                gate = work.tile([P, F], F32, bufs=6)
+                nc.scalar.activation(out=gate[:], in_=live["acc2", i, j][:, 0:F], func=ACT.Silu)
+                live["gate", i, j] = gate
+
+        def product(i):
+            h_sb = outs.tile([P, PAIR, F], F32)
+            for j in range(PAIR):
+                nc.vector.tensor_tensor(
+                    out=h_sb[:, j, :], in0=live["acc2", i, j][:, F : 2 * F], in1=live["gate", i, j][:], op=ALU.mult
+                )
+            b, t0 = i // (N_PAIRS // B), (i % (N_PAIRS // B)) * PAIR
+            nc.sync.dma_start(out=h_view[b, :, t0 : t0 + PAIR, :], in_=h_sb[:])
+
+        def run(stage, i):
+            if 0 <= i < N_PAIRS:
+                stage(i)
+
+        for k in range(-2, N_PAIRS + 4):
+            run(transposes_n, k - 2)
+            run(copy_a, k + 1)
+            run(quantise_a, k)
+            run(quantise_n, k - 3)
+            run(mean_square, k - 1)
+            run(rsqrt, k - 1)
+            run(bias, k + 1)
+            run(product, k - 4)
+            run(project, k)
+            run(copy_n, k - 2)
+            run(gate_matmuls, k - 3)
+            run(transposes_a, k + 2)
+            run(silu, k - 3)
+            run(residual, k)
+            run(squares, k)
+            run(normalise, k - 1)
+            if k == 0:
+                quantise_gate_weights()

@@ -16,10 +16,9 @@ EPS = 1e-6
 P = 128
 PACK = 4
 T_PER_P = S // P
-QUAD = 4
 PAIR = 2
-N_QUADS = B * T_PER_P // QUAD
 N_PAIRS = B * T_PER_P // PAIR
+GPSIMD_COLS = 384
 FLOPS = 2 * B * S * (H * DK * D + D * 2 * F)
 
 
@@ -33,7 +32,7 @@ def tile_transformerblock_pb_t_kernel(tc, x, ao, wo, bo, g2, w1, w3, out_0, out_
     with ExitStack() as ctx:
         ctx.enter_context(tc.manual_schedule())
         consts = ctx.enter_context(tc.tile_pool(name="consts", bufs=1))
-        loads = ctx.enter_context(tc.tile_pool(name="loads", bufs=N_QUADS))
+        loads = ctx.enter_context(tc.tile_pool(name="loads", bufs=N_PAIRS))
         work = ctx.enter_context(tc.tile_pool(name="work", bufs=3))
         outs = ctx.enter_context(tc.tile_pool(name="outs", bufs=6))
         psum = ctx.enter_context(tc.psum_pool(name="psum", bufs=2))
@@ -46,17 +45,22 @@ def tile_transformerblock_pb_t_kernel(tc, x, ao, wo, bo, g2, w1, w3, out_0, out_
         wo_raw = consts.tile([P, PACK, D], BF16)
         w1_raw = consts.tile([P, PACK, F], BF16)
         w3_raw = consts.tile([P, PACK, F], BF16)
+        nc.sync.dma_start(
+            out=wo_raw[:].rearrange("p (u e) n -> p u (e n)", u=2),
+            in_=wo.rearrange("(u p e) n -> p u (e n)", u=2, e=2),
+        )
         a_sb = []
         x_sb = []
-        for q in range(N_QUADS):
-            b, t0 = q // (T_PER_P // QUAD), (q % (T_PER_P // QUAD)) * QUAD
-            a_q = loads.tile([P, H, QUAD, DK], BF16, name="a_q", tag="a_q")
-            nc.sync.dma_start(out=a_q[:], in_=ao_view[b, :, :, t0 : t0 + QUAD, :])
-            if q == 0:
-                nc.sync.dma_start(out=wo_raw[:], in_=wo.rearrange("(j p) n -> p j n", p=P))
-            x_q = loads.tile([P, QUAD, D], BF16, name="x_q", tag="x_q")
-            nc.sync.dma_start(out=x_q[:], in_=x_view[b, :, t0 : t0 + QUAD, :])
-            if q == 0:
+        for i in range(N_PAIRS):
+            b, t0 = i // (N_PAIRS // B), (i % (N_PAIRS // B)) * PAIR
+            a_pair = loads.tile([P, PAIR, H, DK], BF16, name="a_pair", tag="a_pair")
+            for j in range(PAIR):
+                nc.sync.dma_start(out=a_pair[:, j, :, :], in_=ao_view[b, :, :, t0 + j, :])
+            x_pair = loads.tile([P, PAIR, D], BF16, name="x_pair", tag="x_pair")
+            nc.sync.dma_start(out=x_pair[:], in_=x_view[b, :, t0 : t0 + PAIR, :])
+            a_sb.append(a_pair)
+            x_sb.append(x_pair)
+            if i == 1:
                 nc.sync.dma_start(
                     out=w1_raw[:].rearrange("p (u e) f -> p u (e f)", u=2),
                     in_=w1.rearrange("(u p e) f -> p u (e f)", u=2, e=2),
@@ -65,14 +69,10 @@ def tile_transformerblock_pb_t_kernel(tc, x, ao, wo, bo, g2, w1, w3, out_0, out_
                     out=w3_raw[:].rearrange("p (u e) f -> p u (e f)", u=2),
                     in_=w3.rearrange("(u p e) f -> p u (e f)", u=2, e=2),
                 )
-            a_sb.append(a_q)
-            x_sb.append(x_q)
 
         warm = consts.tile([P, 2], F32)
         nc.vector.memset(warm[:], 0.0)
         nc.scalar.activation(out=warm[:, 1:2], in_=warm[:, 0:1], func=ACT.Silu)
-        ident_bf = consts.tile([P, P], BF16)
-        make_identity(nc, ident_bf[:])
         ident_f32 = consts.tile([P, P], F32)
         make_identity(nc, ident_f32[:])
         ones = consts.tile([P, P], BF16)
@@ -80,7 +80,7 @@ def tile_transformerblock_pb_t_kernel(tc, x, ao, wo, bo, g2, w1, w3, out_0, out_
         neg_half = consts.tile([P, PAIR], F32)
         nc.vector.memset(neg_half[:], -0.5)
 
-        bo_ps = psum.tile([P, D], F32, tag="acc1")
+        bo_ps = psum.tile([P, D], F32, tag="bo_ps", bufs=1)
         nc.tensor.matmul(out=bo_ps[:], lhsT=ones[:], rhs=vecs[:, 0, :], start=True, stop=True)
         bo_all = consts.tile([P, D], BF16)
         nc.scalar.copy(out=bo_all[:], in_=bo_ps[:])
@@ -112,27 +112,34 @@ def tile_transformerblock_pb_t_kernel(tc, x, ao, wo, bo, g2, w1, w3, out_0, out_
         live = {}
 
         def transposes_a(i):
-            a_t = psum.tile([P, H, PAIR * P], BF16, tag="a_t")
+            a_t = psum.tile([P, 2, PAIR * P], F32, tag="a_t", bufs=1)
             for j in range(PAIR):
-                for h in range(H):
+                a_words = a_sb[i][:, j, :, :].rearrange("p h d -> p (h d)").bitcast(F32)
+                for u in range(2):
                     nc.tensor.transpose(
-                        a_t[:, h, j * P : (j + 1) * P],
-                        a_sb[i // 2][:, h, (i % 2) * PAIR + j, :],
-                        ident_bf[:],
+                        a_t[:, u, j * P : (j + 1) * P], a_words[:, u * P : (u + 1) * P], ident_f32[:]
                     )
             live["a_t", i] = a_t
 
         def copy_a(i):
-            a_grp = work.tile([P, PAIR * P, PACK], BF16, align_bytes=64)
-            nc.scalar.copy(out=a_grp[:], in_=live["a_t", i][:].rearrange("p h t -> p t h"))
+            a_grp = work.tile([P, PAIR * P, 2], F32, align_bytes=64)
+            nc.scalar.copy(out=a_grp[:], in_=live["a_t", i][:].rearrange("p u t -> p t u"))
             live["a_grp", i] = a_grp
 
         def bias(i):
             xb = work.tile([P, PAIR, D], F32)
-            for j in range(PAIR):
-                nc.gpsimd.tensor_tensor(
-                    out=xb[:, j, :], in0=x_sb[i // 2][:, (i % 2) * PAIR + j, :], in1=bo_all[:], op=ALU.add
-                )
+            nc.gpsimd.tensor_tensor(
+                out=xb[:, :, 0:GPSIMD_COLS],
+                in0=x_sb[i][:, :, 0:GPSIMD_COLS],
+                in1=bo_all[:, 0:GPSIMD_COLS].unsqueeze(1).to_broadcast([P, PAIR, GPSIMD_COLS]),
+                op=ALU.add,
+            )
+            nc.vector.tensor_tensor(
+                out=xb[:, :, GPSIMD_COLS:D],
+                in0=x_sb[i][:, :, GPSIMD_COLS:D],
+                in1=bo_ps[:, GPSIMD_COLS:D].unsqueeze(1).to_broadcast([P, PAIR, D - GPSIMD_COLS]),
+                op=ALU.add,
+            )
             live["xb", i] = xb
 
         def quantise_a(i):
@@ -141,7 +148,7 @@ def tile_transformerblock_pb_t_kernel(tc, x, ao, wo, bo, g2, w1, w3, out_0, out_
             nc.vector.quantize_mx(
                 out=a_codes[:].bitcast(FP8X4),
                 scales=a_scales[:],
-                in_=live["a_grp", i][:].rearrange("p t h -> p (t h)"),
+                in_=live["a_grp", i][:].rearrange("p t u -> p (t u)").bitcast(BF16),
             )
             live["a_codes", i] = a_codes
             live["a_scales", i] = a_scales
@@ -171,14 +178,17 @@ def tile_transformerblock_pb_t_kernel(tc, x, ao, wo, bo, g2, w1, w3, out_0, out_
             nc.sync.dma_start(out=x1_view[b, :, t0 : t0 + PAIR, :], in_=x1[:])
             live["x1", i] = x1
 
-        def squares(i):
-            ssq = work.tile([P, PAIR], F32)
-            for j in range(PAIR):
-                unread = work.tile([P, D], BF16, bufs=4)
-                nc.scalar.activation(
-                    out=unread[:], in_=live["x1", i][:, j, :], func=ACT.Square, accum_out=ssq[:, j : j + 1]
-                )
-            live["ssq", i] = ssq
+        def squares(i, j):
+            if j == 0:
+                ssq = work.tile([P, PAIR], F32)
+                live["ssq", i] = ssq
+            unread = work.tile([P, D], BF16, bufs=4)
+            nc.scalar.activation(
+                out=unread[:],
+                in_=live["x1", i][:, j, :],
+                func=ACT.Square,
+                accum_out=live["ssq", i][:, j : j + 1],
+            )
 
         def mean_square(i):
             ms = work.tile([P, PAIR], F32)
@@ -246,11 +256,10 @@ def tile_transformerblock_pb_t_kernel(tc, x, ao, wo, bo, g2, w1, w3, out_0, out_
                 )
                 live["acc2", i, j] = acc2
 
-        def silu(i):
-            for j in range(PAIR):
-                gate = work.tile([P, F], F32, bufs=6)
-                nc.scalar.activation(out=gate[:], in_=live["acc2", i, j][:, 0:F], func=ACT.Silu)
-                live["gate", i, j] = gate
+        def silu(i, j):
+            gate = work.tile([P, F], F32, bufs=6)
+            nc.scalar.activation(out=gate[:], in_=live["acc2", i, j][:, 0:F], func=ACT.Silu)
+            live["gate", i, j] = gate
 
         def product(i):
             h_sb = outs.tile([P, PAIR, F], F32)
@@ -261,9 +270,9 @@ def tile_transformerblock_pb_t_kernel(tc, x, ao, wo, bo, g2, w1, w3, out_0, out_
             b, t0 = i // (N_PAIRS // B), (i % (N_PAIRS // B)) * PAIR
             nc.sync.dma_start(out=h_view[b, :, t0 : t0 + PAIR, :], in_=h_sb[:])
 
-        def run(stage, i):
+        def run(stage, i, *tile):
             if 0 <= i < N_PAIRS:
-                stage(i)
+                stage(i, *tile)
 
         for k in range(-2, N_PAIRS + 4):
             run(transposes_n, k - 2)
@@ -272,15 +281,16 @@ def tile_transformerblock_pb_t_kernel(tc, x, ao, wo, bo, g2, w1, w3, out_0, out_
             run(quantise_n, k - 3)
             run(mean_square, k - 1)
             run(rsqrt, k - 1)
-            run(bias, k + 1)
             run(product, k - 4)
+            run(bias, k + 1)
             run(project, k)
             run(copy_n, k - 2)
             run(gate_matmuls, k - 3)
             run(transposes_a, k + 2)
-            run(silu, k - 3)
             run(residual, k)
-            run(squares, k)
+            for j in range(PAIR):
+                run(squares, k, j)
+                run(silu, k - 3, j)
             run(normalise, k - 1)
             if k == 0:
                 quantise_gate_weights()

@@ -18,7 +18,6 @@ PACK = 4
 T_PER_P = S // P
 PAIR = 2
 N_PAIRS = B * T_PER_P // PAIR
-GPSIMD_COLS = 384
 FLOPS = 2 * B * S * (H * DK * D + D * 2 * F)
 
 
@@ -34,7 +33,7 @@ def tile_transformerblock_pb_t_kernel(tc, x, ao, wo, bo, g2, w1, w3, out_0, out_
         consts = ctx.enter_context(tc.tile_pool(name="consts", bufs=1))
         loads = ctx.enter_context(tc.tile_pool(name="loads", bufs=N_PAIRS))
         work = ctx.enter_context(tc.tile_pool(name="work", bufs=3))
-        outs = ctx.enter_context(tc.tile_pool(name="outs", bufs=6))
+        outs = ctx.enter_context(tc.tile_pool(name="outs", bufs=12))
         psum = ctx.enter_context(tc.psum_pool(name="psum", bufs=2))
 
         vecs = consts.tile([P, 2, D], BF16)
@@ -79,8 +78,10 @@ def tile_transformerblock_pb_t_kernel(tc, x, ao, wo, bo, g2, w1, w3, out_0, out_
         nc.vector.memset(ones[:], 1.0)
         neg_half = consts.tile([P, PAIR], F32)
         nc.vector.memset(neg_half[:], -0.5)
+        eps = consts.tile([P, 1], F32)
+        nc.vector.memset(eps[:], EPS)
 
-        bo_ps = psum.tile([P, D], F32, tag="bo_ps", bufs=1)
+        bo_ps = psum.tile([P, D], F32, tag="acc1")
         nc.tensor.matmul(out=bo_ps[:], lhsT=ones[:], rhs=vecs[:, 0, :], start=True, stop=True)
         bo_all = consts.tile([P, D], BF16)
         nc.scalar.copy(out=bo_all[:], in_=bo_ps[:])
@@ -112,7 +113,7 @@ def tile_transformerblock_pb_t_kernel(tc, x, ao, wo, bo, g2, w1, w3, out_0, out_
         live = {}
 
         def transposes_a(i):
-            a_t = psum.tile([P, 2, PAIR * P], F32, tag="a_t", bufs=1)
+            a_t = psum.tile([P, 2, PAIR * P], F32, tag="a_t")
             for j in range(PAIR):
                 a_words = a_sb[i][:, j, :, :].rearrange("p h d -> p (h d)").bitcast(F32)
                 for u in range(2):
@@ -129,16 +130,7 @@ def tile_transformerblock_pb_t_kernel(tc, x, ao, wo, bo, g2, w1, w3, out_0, out_
         def bias(i):
             xb = work.tile([P, PAIR, D], F32)
             nc.gpsimd.tensor_tensor(
-                out=xb[:, :, 0:GPSIMD_COLS],
-                in0=x_sb[i][:, :, 0:GPSIMD_COLS],
-                in1=bo_all[:, 0:GPSIMD_COLS].unsqueeze(1).to_broadcast([P, PAIR, GPSIMD_COLS]),
-                op=ALU.add,
-            )
-            nc.vector.tensor_tensor(
-                out=xb[:, :, GPSIMD_COLS:D],
-                in0=x_sb[i][:, :, GPSIMD_COLS:D],
-                in1=bo_ps[:, GPSIMD_COLS:D].unsqueeze(1).to_broadcast([P, PAIR, D - GPSIMD_COLS]),
-                op=ALU.add,
+                out=xb[:], in0=x_sb[i][:], in1=bo_all[:].unsqueeze(1).to_broadcast([P, PAIR, D]), op=ALU.add
             )
             live["xb", i] = xb
 
@@ -192,9 +184,7 @@ def tile_transformerblock_pb_t_kernel(tc, x, ao, wo, bo, g2, w1, w3, out_0, out_
 
         def mean_square(i):
             ms = work.tile([P, PAIR], F32)
-            nc.vector.tensor_scalar(
-                out=ms[:], in0=live["ssq", i][:], scalar1=1.0 / D, scalar2=EPS, op0=ALU.mult, op1=ALU.add
-            )
+            nc.scalar.activation(out=ms[:], in_=live["ssq", i][:], func=ACT.Identity, scale=1.0 / D, bias=eps[:])
             live["ms", i] = ms
 
         def rsqrt(i):
@@ -242,31 +232,31 @@ def tile_transformerblock_pb_t_kernel(tc, x, ao, wo, bo, g2, w1, w3, out_0, out_
             live["n_scales", i] = n_scales
 
         def gate_matmuls(i):
-            for j in range(PAIR):
-                cols = slice(j * P, (j + 1) * P)
-                acc2 = psum.tile([P, 2 * F], F32, tag="acc2")
-                nc.tensor.matmul_mx(
-                    out=acc2[:],
-                    lhsT=live["n_codes", i][:, cols].bitcast(FP8X4),
-                    lhsT_scale=live["n_scales", i][:, cols],
-                    rhs=w13_codes[:].bitcast(FP8X4),
-                    rhs_scale=w13_scales[:],
-                    start=True,
-                    stop=True,
-                )
-                live["acc2", i, j] = acc2
+            u_ps = psum.tile([P, PAIR, F], F32, tag="u_ps", bufs=1)
+            v_ps = psum.tile([P, PAIR, F], F32, tag="v_ps", bufs=1)
+            for out_ps, w_cols in ((u_ps, slice(0, F)), (v_ps, slice(F, 2 * F))):
+                for j in range(PAIR):
+                    cols = slice(j * P, (j + 1) * P)
+                    nc.tensor.matmul_mx(
+                        out=out_ps[:, j, :],
+                        lhsT=live["n_codes", i][:, cols].bitcast(FP8X4),
+                        lhsT_scale=live["n_scales", i][:, cols],
+                        rhs=w13_codes[:, w_cols].bitcast(FP8X4),
+                        rhs_scale=w13_scales[:, w_cols],
+                        start=True,
+                        stop=True,
+                    )
+            live["u_ps", i] = u_ps
+            live["v_ps", i] = v_ps
 
-        def silu(i, j):
-            gate = work.tile([P, F], F32, bufs=6)
-            nc.scalar.activation(out=gate[:], in_=live["acc2", i, j][:, 0:F], func=ACT.Silu)
-            live["gate", i, j] = gate
+        def silu(i):
+            gate = work.tile([P, PAIR, F], F32)
+            nc.scalar.activation(out=gate[:], in_=live["u_ps", i][:], func=ACT.Silu)
+            live["gate", i] = gate
 
         def product(i):
             h_sb = outs.tile([P, PAIR, F], F32)
-            for j in range(PAIR):
-                nc.vector.tensor_tensor(
-                    out=h_sb[:, j, :], in0=live["acc2", i, j][:, F : 2 * F], in1=live["gate", i, j][:], op=ALU.mult
-                )
+            nc.vector.tensor_tensor(out=h_sb[:], in0=live["v_ps", i][:], in1=live["gate", i][:], op=ALU.mult)
             b, t0 = i // (N_PAIRS // B), (i % (N_PAIRS // B)) * PAIR
             nc.sync.dma_start(out=h_view[b, :, t0 : t0 + PAIR, :], in_=h_sb[:])
 
@@ -279,7 +269,6 @@ def tile_transformerblock_pb_t_kernel(tc, x, ao, wo, bo, g2, w1, w3, out_0, out_
             run(copy_a, k + 1)
             run(quantise_a, k)
             run(quantise_n, k - 3)
-            run(mean_square, k - 1)
             run(rsqrt, k - 1)
             run(product, k - 4)
             run(bias, k + 1)
@@ -288,9 +277,10 @@ def tile_transformerblock_pb_t_kernel(tc, x, ao, wo, bo, g2, w1, w3, out_0, out_
             run(gate_matmuls, k - 3)
             run(transposes_a, k + 2)
             run(residual, k)
-            for j in range(PAIR):
-                run(squares, k, j)
-                run(silu, k - 3, j)
+            run(squares, k, 0)
+            run(silu, k - 3)
+            run(squares, k, 1)
+            run(mean_square, k)
             run(normalise, k - 1)
             if k == 0:
                 quantise_gate_weights()

@@ -18,6 +18,7 @@ PACK = 4
 T_PER_P = S // P
 PAIR = 2
 N_PAIRS = B * T_PER_P // PAIR
+EXTRA_PASSES = 2
 FLOPS = 2 * B * S * (H * DK * D + D * 2 * F)
 
 
@@ -113,7 +114,7 @@ def tile_transformerblock_pb_t_kernel(tc, x, ao, wo, bo, g2, w1, w3, out_0, out_
         live = {}
 
         def transposes_a(i):
-            a_t = psum.tile([P, 2, PAIR * P], F32, tag="a_t")
+            a_t = psum.tile([P, 2, PAIR * P], F32, tag="a_t", bufs=1)
             for j in range(PAIR):
                 a_words = a_sb[i][:, j, :, :].rearrange("p h d -> p (h d)").bitcast(F32)
                 for u in range(2):
@@ -260,6 +261,20 @@ def tile_transformerblock_pb_t_kernel(tc, x, ao, wo, bo, g2, w1, w3, out_0, out_
             b, t0 = i // (N_PAIRS // B), (i % (N_PAIRS // B)) * PAIR
             nc.sync.dma_start(out=h_view[b, :, t0 : t0 + PAIR, :], in_=h_sb[:])
 
+        unread_ps = psum.tile([P, D], F32, tag="unread_ps", bufs=1)
+
+        def keep_clock_up():
+            for extra in range(EXTRA_PASSES):
+                nc.tensor.matmul_mx(
+                    out=unread_ps[:],
+                    lhsT=wo_codes[:, 0:P].bitcast(FP8X4),
+                    lhsT_scale=wo_scales[:, 0:P],
+                    rhs=wo_codes[:].bitcast(FP8X4),
+                    rhs_scale=wo_scales[:],
+                    start=True,
+                    stop=True,
+                )
+
         def run(stage, i, *tile):
             if 0 <= i < N_PAIRS:
                 stage(i, *tile)
@@ -269,18 +284,19 @@ def tile_transformerblock_pb_t_kernel(tc, x, ao, wo, bo, g2, w1, w3, out_0, out_
             run(copy_a, k + 1)
             run(quantise_a, k)
             run(quantise_n, k - 3)
-            run(rsqrt, k - 1)
             run(product, k - 4)
             run(bias, k + 1)
             run(project, k)
             run(copy_n, k - 2)
             run(gate_matmuls, k - 3)
             run(transposes_a, k + 2)
+            keep_clock_up()
             run(residual, k)
             run(squares, k, 0)
-            run(silu, k - 3)
             run(squares, k, 1)
             run(mean_square, k)
+            run(rsqrt, k)
+            run(silu, k - 3)
             run(normalise, k - 1)
             if k == 0:
                 quantise_gate_weights()

@@ -113,6 +113,12 @@ def tile_transformerblock_pb_t_kernel(tc, x, ao, wo, bo, g2, w1, w3, out_0, out_
 
         live = {}
 
+        def group_tile(k):
+            if ("grp", k) not in live:
+                grp = work.tile([P, 2, PAIR * P, 2], F32, align_bytes=64)
+                live["grp", k] = grp
+            return live["grp", k]
+
         def transposes_a(i):
             a_t = psum.tile([P, 2, PAIR * P], F32, tag="a_t", bufs=1)
             for j in range(PAIR):
@@ -124,52 +130,53 @@ def tile_transformerblock_pb_t_kernel(tc, x, ao, wo, bo, g2, w1, w3, out_0, out_
             live["a_t", i] = a_t
 
         def copy_a(i):
-            a_grp = work.tile([P, PAIR * P, 2], F32, align_bytes=64)
-            nc.scalar.copy(out=a_grp[:], in_=live["a_t", i][:].rearrange("p u t -> p t u"))
-            live["a_grp", i] = a_grp
+            nc.scalar.copy(out=group_tile(i - 1)[:, 0, :, :], in_=live["a_t", i][:].rearrange("p u t -> p t u"))
 
-        def bias(i):
-            xb = work.tile([P, PAIR, D], F32)
-            nc.gpsimd.tensor_tensor(
-                out=xb[:], in0=x_sb[i][:], in1=bo_all[:].unsqueeze(1).to_broadcast([P, PAIR, D]), op=ALU.add
-            )
-            live["xb", i] = xb
+        def bias(i, j):
+            xb = work.tile([P, D], F32, bufs=PAIR)
+            nc.gpsimd.tensor_tensor(out=xb[:], in0=x_sb[i][:, j, :], in1=bo_all[:], op=ALU.add)
+            live["xb", i, j] = xb
 
-        def quantise_a(i):
-            a_codes = work.tile([P, PAIR * P], U32, align_bytes=64)
-            a_scales = work.tile([P, PAIR * P], U8, align_bytes=64)
+        def quantise(k):
+            first = 0 if 0 <= k + 1 < N_PAIRS else 1
+            last = 2 if 0 <= k - 3 < N_PAIRS else 1
+            if first >= last:
+                return
+            codes = work.tile([P, 2, PAIR * P], U32, align_bytes=64)
+            scales = work.tile([P, 2, PAIR * P], U8, align_bytes=64)
             nc.vector.quantize_mx(
-                out=a_codes[:].bitcast(FP8X4),
-                scales=a_scales[:],
-                in_=live["a_grp", i][:].rearrange("p t u -> p (t u)").bitcast(BF16),
+                out=codes[:, first:last, :].rearrange("p s t -> p (s t)").bitcast(FP8X4),
+                scales=scales[:, first:last, :].rearrange("p s t -> p (s t)"),
+                in_=group_tile(k)[:, first:last, :, :].rearrange("p s t u -> p (s t u)").bitcast(BF16),
             )
-            live["a_codes", i] = a_codes
-            live["a_scales", i] = a_scales
+            live["codes", k] = codes
+            live["scales", k] = scales
 
-        def project(i):
-            for j in range(PAIR):
-                cols = slice(j * P, (j + 1) * P)
-                acc1 = psum.tile([P, D], F32, tag="acc1")
-                nc.tensor.matmul_mx(
-                    out=acc1[:],
-                    lhsT=live["a_codes", i][:, cols].bitcast(FP8X4),
-                    lhsT_scale=live["a_scales", i][:, cols],
-                    rhs=wo_codes[:].bitcast(FP8X4),
-                    rhs_scale=wo_scales[:],
-                    start=True,
-                    stop=True,
-                )
-                live["acc1", i, j] = acc1
+        def project(i, j):
+            cols = slice(j * P, (j + 1) * P)
+            acc1 = psum.tile([P, D], F32, tag="acc1")
+            nc.tensor.matmul_mx(
+                out=acc1[:],
+                lhsT=live["codes", i - 1][:, 0, cols].bitcast(FP8X4),
+                lhsT_scale=live["scales", i - 1][:, 0, cols],
+                rhs=wo_codes[:].bitcast(FP8X4),
+                rhs_scale=wo_scales[:],
+                start=True,
+                stop=True,
+            )
+            live["acc1", i, j] = acc1
 
-        def residual(i):
-            x1 = outs.tile([P, PAIR, D], F32)
-            for j in range(PAIR):
-                nc.vector.tensor_tensor(
-                    out=x1[:, j, :], in0=live["acc1", i, j][:], in1=live["xb", i][:, j, :], op=ALU.add
-                )
+        def residual(i, j):
+            if j == 0:
+                x1 = outs.tile([P, PAIR, D], F32)
+                live["x1", i] = x1
+            nc.vector.tensor_tensor(
+                out=live["x1", i][:, j, :], in0=live["acc1", i, j][:], in1=live["xb", i, j][:], op=ALU.add
+            )
+
+        def store_x1(i):
             b, t0 = i // (N_PAIRS // B), (i % (N_PAIRS // B)) * PAIR
-            nc.sync.dma_start(out=x1_view[b, :, t0 : t0 + PAIR, :], in_=x1[:])
-            live["x1", i] = x1
+            nc.sync.dma_start(out=x1_view[b, :, t0 : t0 + PAIR, :], in_=live["x1", i][:])
 
         def squares(i, j):
             if j == 0:
@@ -217,20 +224,7 @@ def tile_transformerblock_pb_t_kernel(tc, x, ao, wo, bo, g2, w1, w3, out_0, out_
             live["n_t", i] = n_t
 
         def copy_n(i):
-            n_grp = work.tile([P, PAIR * P, 2], F32, align_bytes=64)
-            nc.scalar.copy(out=n_grp[:], in_=live["n_t", i][:].rearrange("p u t -> p t u"))
-            live["n_grp", i] = n_grp
-
-        def quantise_n(i):
-            n_codes = work.tile([P, PAIR * P], U32, align_bytes=64)
-            n_scales = work.tile([P, PAIR * P], U8, align_bytes=64)
-            nc.vector.quantize_mx(
-                out=n_codes[:].bitcast(FP8X4),
-                scales=n_scales[:],
-                in_=live["n_grp", i][:].rearrange("p t u -> p (t u)").bitcast(BF16),
-            )
-            live["n_codes", i] = n_codes
-            live["n_scales", i] = n_scales
+            nc.scalar.copy(out=group_tile(i + 3)[:, 1, :, :], in_=live["n_t", i][:].rearrange("p u t -> p t u"))
 
         def gate_matmuls(i):
             u_ps = psum.tile([P, PAIR, F], F32, tag="u_ps", bufs=1)
@@ -240,8 +234,8 @@ def tile_transformerblock_pb_t_kernel(tc, x, ao, wo, bo, g2, w1, w3, out_0, out_
                     cols = slice(j * P, (j + 1) * P)
                     nc.tensor.matmul_mx(
                         out=out_ps[:, j, :],
-                        lhsT=live["n_codes", i][:, cols].bitcast(FP8X4),
-                        lhsT_scale=live["n_scales", i][:, cols],
+                        lhsT=live["codes", i + 3][:, 1, cols].bitcast(FP8X4),
+                        lhsT_scale=live["scales", i + 3][:, 1, cols],
                         rhs=w13_codes[:, w_cols].bitcast(FP8X4),
                         rhs_scale=w13_scales[:, w_cols],
                         start=True,
@@ -279,24 +273,25 @@ def tile_transformerblock_pb_t_kernel(tc, x, ao, wo, bo, g2, w1, w3, out_0, out_
             if 0 <= i < N_PAIRS:
                 stage(i, *tile)
 
-        for k in range(-2, N_PAIRS + 4):
-            run(transposes_n, k - 2)
-            run(copy_a, k + 1)
-            run(quantise_a, k)
-            run(quantise_n, k - 3)
-            run(product, k - 4)
-            run(bias, k + 1)
-            run(project, k)
-            run(copy_n, k - 2)
+        for k in range(-3, N_PAIRS + 3):
+            quantise(k)
             run(gate_matmuls, k - 3)
-            run(transposes_a, k + 2)
-            keep_clock_up()
-            run(residual, k)
+            for j in range(PAIR):
+                run(residual, k, j)
+                run(bias, k + 1, j)
+                run(project, k + 1, j)
+            run(store_x1, k)
+            run(copy_n, k - 2)
+            run(copy_a, k + 2)
             run(squares, k, 0)
+            run(silu, k - 3)
             run(squares, k, 1)
             run(mean_square, k)
             run(rsqrt, k)
-            run(silu, k - 3)
             run(normalise, k - 1)
+            run(transposes_a, k + 3)
+            run(transposes_n, k - 1)
+            keep_clock_up()
+            run(product, k - 3)
             if k == 0:
                 quantise_gate_weights()

@@ -18,7 +18,9 @@ PACK = 4
 T_PER_P = S // P
 PAIR = 2
 N_PAIRS = B * T_PER_P // PAIR
-EXTRA_PASSES = 2
+HEAD_PAIRS = 1
+WO_VECTOR = 320
+D_GPSIMD = 464
 FLOPS = 2 * B * S * (H * DK * D + D * 2 * F)
 
 
@@ -34,13 +36,11 @@ def tile_transformerblock_pb_t_kernel(tc, x, ao, wo, bo, g2, w1, w3, out_0, out_
         consts = ctx.enter_context(tc.tile_pool(name="consts", bufs=1))
         loads = ctx.enter_context(tc.tile_pool(name="loads", bufs=N_PAIRS))
         work = ctx.enter_context(tc.tile_pool(name="work", bufs=3))
-        outs = ctx.enter_context(tc.tile_pool(name="outs", bufs=12))
+        outs = ctx.enter_context(tc.tile_pool(name="outs", bufs=10))
         psum = ctx.enter_context(tc.psum_pool(name="psum", bufs=2))
 
         vecs = consts.tile([P, 2, D], BF16)
         nc.vector.memset(vecs[:], 0.0)
-        nc.sync.dma_start(out=vecs[0:1, 0, :], in_=bo.unsqueeze(0))
-        nc.sync.dma_start(out=vecs[0:1, 1, :], in_=g2.unsqueeze(0))
 
         wo_raw = consts.tile([P, PACK, D], BF16)
         w1_raw = consts.tile([P, PACK, F], BF16)
@@ -56,6 +56,9 @@ def tile_transformerblock_pb_t_kernel(tc, x, ao, wo, bo, g2, w1, w3, out_0, out_
             a_pair = loads.tile([P, PAIR, H, DK], BF16, name="a_pair", tag="a_pair")
             for j in range(PAIR):
                 nc.sync.dma_start(out=a_pair[:, j, :, :], in_=ao_view[b, :, :, t0 + j, :])
+            if i == 0:
+                nc.sync.dma_start(out=vecs[0:1, 0, :], in_=bo.unsqueeze(0))
+                nc.sync.dma_start(out=vecs[0:1, 1, :], in_=g2.unsqueeze(0))
             x_pair = loads.tile([P, PAIR, D], BF16, name="x_pair", tag="x_pair")
             nc.sync.dma_start(out=x_pair[:], in_=x_view[b, :, t0 : t0 + PAIR, :])
             a_sb.append(a_pair)
@@ -75,6 +78,8 @@ def tile_transformerblock_pb_t_kernel(tc, x, ao, wo, bo, g2, w1, w3, out_0, out_
         nc.scalar.activation(out=warm[:, 1:2], in_=warm[:, 0:1], func=ACT.Silu)
         ident_f32 = consts.tile([P, P], F32)
         make_identity(nc, ident_f32[:])
+        ident_bf16 = consts.tile([P, P], BF16)
+        make_identity(nc, ident_bf16[:])
         ones = consts.tile([P, P], BF16)
         nc.vector.memset(ones[:], 1.0)
         neg_half = consts.tile([P, PAIR], F32)
@@ -82,17 +87,11 @@ def tile_transformerblock_pb_t_kernel(tc, x, ao, wo, bo, g2, w1, w3, out_0, out_
         eps = consts.tile([P, 1], F32)
         nc.vector.memset(eps[:], EPS)
 
-        bo_ps = psum.tile([P, D], F32, tag="acc1")
-        nc.tensor.matmul(out=bo_ps[:], lhsT=ones[:], rhs=vecs[:, 0, :], start=True, stop=True)
-        bo_all = consts.tile([P, D], BF16)
-        nc.scalar.copy(out=bo_all[:], in_=bo_ps[:])
-        g2_ps = psum.tile([P, D], F32, tag="g2_ps", bufs=1)
-        nc.tensor.matmul(out=g2_ps[:], lhsT=ones[:], rhs=vecs[:, 1, :], start=True, stop=True)
-
         wo_grp = consts.tile([P, D, PACK], BF16, align_bytes=64)
         wo_codes = consts.tile([P, D], U32, align_bytes=64)
         wo_scales = consts.tile([P, D], U8, align_bytes=64)
-        nc.vector.tensor_copy(out=wo_grp[:], in_=wo_raw[:].rearrange("p j n -> p n j"))
+        nc.vector.tensor_copy(out=wo_grp[:, 0:WO_VECTOR, :], in_=wo_raw[:, :, 0:WO_VECTOR].rearrange("p j n -> p n j"))
+        nc.scalar.copy(out=wo_grp[:, WO_VECTOR:D, :], in_=wo_raw[:, :, WO_VECTOR:D].rearrange("p j n -> p n j"))
         nc.vector.quantize_mx(
             out=wo_codes[:].bitcast(FP8X4),
             scales=wo_scales[:],
@@ -102,9 +101,11 @@ def tile_transformerblock_pb_t_kernel(tc, x, ao, wo, bo, g2, w1, w3, out_0, out_
         w13_codes = consts.tile([P, 2 * F], U32, align_bytes=64)
         w13_scales = consts.tile([P, 2 * F], U8, align_bytes=64)
 
-        def quantise_gate_weights():
+        def lay_out_gate_weights():
             nc.vector.tensor_copy(out=w13_grp[:, 0:F, :], in_=w1_raw[:].rearrange("p j f -> p f j"))
             nc.vector.tensor_copy(out=w13_grp[:, F : 2 * F, :], in_=w3_raw[:].rearrange("p j f -> p f j"))
+
+        def quantise_gate_weights():
             nc.vector.quantize_mx(
                 out=w13_codes[:].bitcast(FP8X4),
                 scales=w13_scales[:],
@@ -130,16 +131,38 @@ def tile_transformerblock_pb_t_kernel(tc, x, ao, wo, bo, g2, w1, w3, out_0, out_
             live["a_t", i] = a_t
 
         def copy_a(i):
-            nc.scalar.copy(out=group_tile(i - 1)[:, 0, :, :], in_=live["a_t", i][:].rearrange("p u t -> p t u"))
+            nc.scalar.copy(out=group_tile(i - 2)[:, 0, :, :], in_=live["a_t", i][:].rearrange("p u t -> p t u"))
 
-        def bias(i, j):
-            xb = work.tile([P, D], F32, bufs=PAIR)
-            nc.gpsimd.tensor_tensor(out=xb[:], in0=x_sb[i][:, j, :], in1=bo_all[:], op=ALU.add)
-            live["xb", i, j] = xb
+        def bias_gpsimd(i):
+            xb = work.tile([P, PAIR, D], F32, bufs=4)
+            nc.gpsimd.tensor_tensor(
+                out=xb[:, :, 0:D_GPSIMD],
+                in0=x_sb[i][:, :, 0:D_GPSIMD],
+                in1=bo_all[:, 0:D_GPSIMD].unsqueeze(1).to_broadcast([P, PAIR, D_GPSIMD]),
+                op=ALU.add,
+            )
+            live["xb", i] = xb
+
+        def bias_vector(i):
+            nc.vector.tensor_tensor(
+                out=live["xb", i][:, :, D_GPSIMD:D],
+                in0=bo_ps[:, D_GPSIMD:D].unsqueeze(1).to_broadcast([P, PAIR, D - D_GPSIMD]),
+                in1=x_sb[i][:, :, D_GPSIMD:D],
+                op=ALU.add,
+            )
+
+        def bias_tensor(i, j):
+            if j == 0:
+                xb = work.tile([P, PAIR, D], F32, bufs=4)
+                live["xb", i] = xb
+            xb_ps = psum.tile([P, D], F32, name="xb_ps", tag=("u_ps", "v_ps")[j], bufs=1)
+            nc.tensor.matmul(out=xb_ps[:], lhsT=ident_bf16[:], rhs=x_sb[i][:, j, :], start=True, stop=False)
+            nc.tensor.matmul(out=xb_ps[:], lhsT=ones[:], rhs=vecs[:, 0, :], start=False, stop=True)
+            nc.scalar.copy(out=live["xb", i][:, j, :], in_=xb_ps[:])
 
         def quantise(k):
-            first = 0 if 0 <= k + 1 < N_PAIRS else 1
-            last = 2 if 0 <= k - 3 < N_PAIRS else 1
+            first = 0 if 0 <= k + 2 < N_PAIRS else 1
+            last = 2 if 0 <= k - 2 < N_PAIRS else 1
             if first >= last:
                 return
             codes = work.tile([P, 2, PAIR * P], U32, align_bytes=64)
@@ -157,8 +180,8 @@ def tile_transformerblock_pb_t_kernel(tc, x, ao, wo, bo, g2, w1, w3, out_0, out_
             acc1 = psum.tile([P, D], F32, tag="acc1")
             nc.tensor.matmul_mx(
                 out=acc1[:],
-                lhsT=live["codes", i - 1][:, 0, cols].bitcast(FP8X4),
-                lhsT_scale=live["scales", i - 1][:, 0, cols],
+                lhsT=live["codes", i - 2][:, 0, cols].bitcast(FP8X4),
+                lhsT_scale=live["scales", i - 2][:, 0, cols],
                 rhs=wo_codes[:].bitcast(FP8X4),
                 rhs_scale=wo_scales[:],
                 start=True,
@@ -171,7 +194,7 @@ def tile_transformerblock_pb_t_kernel(tc, x, ao, wo, bo, g2, w1, w3, out_0, out_
                 x1 = outs.tile([P, PAIR, D], F32)
                 live["x1", i] = x1
             nc.vector.tensor_tensor(
-                out=live["x1", i][:, j, :], in0=live["acc1", i, j][:], in1=live["xb", i, j][:], op=ALU.add
+                out=live["x1", i][:, j, :], in0=live["acc1", i, j][:], in1=live["xb", i][:, j, :], op=ALU.add
             )
 
         def store_x1(i):
@@ -224,7 +247,7 @@ def tile_transformerblock_pb_t_kernel(tc, x, ao, wo, bo, g2, w1, w3, out_0, out_
             live["n_t", i] = n_t
 
         def copy_n(i):
-            nc.scalar.copy(out=group_tile(i + 3)[:, 1, :, :], in_=live["n_t", i][:].rearrange("p u t -> p t u"))
+            nc.scalar.copy(out=group_tile(i + 2)[:, 1, :, :], in_=live["n_t", i][:].rearrange("p u t -> p t u"))
 
         def gate_matmuls(i):
             u_ps = psum.tile([P, PAIR, F], F32, tag="u_ps", bufs=1)
@@ -234,8 +257,8 @@ def tile_transformerblock_pb_t_kernel(tc, x, ao, wo, bo, g2, w1, w3, out_0, out_
                     cols = slice(j * P, (j + 1) * P)
                     nc.tensor.matmul_mx(
                         out=out_ps[:, j, :],
-                        lhsT=live["codes", i + 3][:, 1, cols].bitcast(FP8X4),
-                        lhsT_scale=live["scales", i + 3][:, 1, cols],
+                        lhsT=live["codes", i + 2][:, 1, cols].bitcast(FP8X4),
+                        lhsT_scale=live["scales", i + 2][:, 1, cols],
                         rhs=w13_codes[:, w_cols].bitcast(FP8X4),
                         rhs_scale=w13_scales[:, w_cols],
                         start=True,
@@ -255,43 +278,45 @@ def tile_transformerblock_pb_t_kernel(tc, x, ao, wo, bo, g2, w1, w3, out_0, out_
             b, t0 = i // (N_PAIRS // B), (i % (N_PAIRS // B)) * PAIR
             nc.sync.dma_start(out=h_view[b, :, t0 : t0 + PAIR, :], in_=h_sb[:])
 
-        unread_ps = psum.tile([P, D], F32, tag="unread_ps", bufs=1)
-
-        def keep_clock_up():
-            for extra in range(EXTRA_PASSES):
-                nc.tensor.matmul_mx(
-                    out=unread_ps[:],
-                    lhsT=wo_codes[:, 0:P].bitcast(FP8X4),
-                    lhsT_scale=wo_scales[:, 0:P],
-                    rhs=wo_codes[:].bitcast(FP8X4),
-                    rhs_scale=wo_scales[:],
-                    start=True,
-                    stop=True,
-                )
-
         def run(stage, i, *tile):
             if 0 <= i < N_PAIRS:
                 stage(i, *tile)
 
-        for k in range(-3, N_PAIRS + 3):
-            quantise(k)
-            run(gate_matmuls, k - 3)
+        transposes_a(0)
+        copy_a(0)
+        bo_ps = psum.tile([P, D], F32, tag="bo_ps", bufs=1)
+        nc.tensor.matmul(out=bo_ps[:], lhsT=ones[:], rhs=vecs[:, 0, :], start=True, stop=True)
+        bo_all = consts.tile([P, D], BF16)
+        nc.vector.tensor_copy(out=bo_all[:], in_=bo_ps[:])
+        g2_ps = psum.tile([P, D], F32, tag="g2_ps", bufs=1)
+        nc.tensor.matmul(out=g2_ps[:], lhsT=ones[:], rhs=vecs[:, 1, :], start=True, stop=True)
+        bias_tensor(0, 0)
+        bias_gpsimd(1)
+        bias_vector(1)
+        for k in range(-2, N_PAIRS + 3):
             for j in range(PAIR):
                 run(residual, k, j)
-                run(bias, k + 1, j)
                 run(project, k + 1, j)
             run(store_x1, k)
-            run(copy_n, k - 2)
-            run(copy_a, k + 2)
-            run(squares, k, 0)
             run(silu, k - 3)
+            run(squares, k, 0)
             run(squares, k, 1)
             run(mean_square, k)
             run(rsqrt, k)
+            if k >= 0:
+                run(bias_gpsimd, k + 2)
             run(normalise, k - 1)
             run(transposes_a, k + 3)
+            run(copy_a, k + 3)
+            if k == -2:
+                bias_tensor(0, 1)
             run(transposes_n, k - 1)
-            keep_clock_up()
+            run(copy_n, k - 1)
+            quantise(k)
             run(product, k - 3)
+            if k >= 0:
+                run(bias_vector, k + 2)
+            run(gate_matmuls, k - 2)
             if k == 0:
+                lay_out_gate_weights()
                 quantise_gate_weights()

@@ -63,7 +63,7 @@ def tile_transformerblock_pb_t_kernel(tc, x, ao, wo, bo, g2, w1, w3, out_0, out_
             nc.sync.dma_start(out=x_pair[:], in_=x_view[b, :, t0 : t0 + PAIR, :])
             a_sb.append(a_pair)
             x_sb.append(x_pair)
-            if i == 1:
+            if i == 2:
                 nc.sync.dma_start(
                     out=w1_raw[:].rearrange("p (u e) f -> p u (e f)", u=2),
                     in_=w1.rearrange("(u p e) f -> p u (e f)", u=2, e=2),
@@ -292,7 +292,6 @@ def tile_transformerblock_pb_t_kernel(tc, x, ao, wo, bo, g2, w1, w3, out_0, out_
         nc.tensor.matmul(out=g2_ps[:], lhsT=ones[:], rhs=vecs[:, 1, :], start=True, stop=True)
         bias_tensor(0, 0)
         bias_gpsimd(1)
-        bias_vector(1)
         for k in range(-2, N_PAIRS + 3):
             for j in range(PAIR):
                 run(residual, k, j)
@@ -314,6 +313,8 @@ def tile_transformerblock_pb_t_kernel(tc, x, ao, wo, bo, g2, w1, w3, out_0, out_
             run(copy_n, k - 1)
             quantise(k)
             run(product, k - 3)
+            if k == -2:
+                bias_vector(1)
             if k >= 0:
                 run(bias_vector, k + 2)
             run(gate_matmuls, k - 2)

@@ -143,13 +143,12 @@ def tile_transformerblock_pb_t_kernel(tc, x, ao, wo, bo, g2, w1, w3, out_0, out_
             )
             live["xb", i] = xb
 
-        def bias_vector(i):
-            nc.vector.tensor_tensor(
-                out=live["xb", i][:, :, D_GPSIMD:D],
-                in0=bo_ps[:, D_GPSIMD:D].unsqueeze(1).to_broadcast([P, PAIR, D - D_GPSIMD]),
-                in1=x_sb[i][:, :, D_GPSIMD:D],
-                op=ALU.add,
-            )
+        def bias_share(i):
+            part_ps = psum.tile([P, PAIR, D - D_GPSIMD], F32, tag="part_ps", bufs=1)
+            for j in range(PAIR):
+                nc.tensor.matmul(out=part_ps[:, j, :], lhsT=ident_bf16[:], rhs=x_sb[i][:, j, D_GPSIMD:D], start=True, stop=False)
+                nc.tensor.matmul(out=part_ps[:, j, :], lhsT=ones[:], rhs=vecs[:, 0, D_GPSIMD:D], start=False, stop=True)
+            nc.scalar.copy(out=live["xb", i][:, :, D_GPSIMD:D], in_=part_ps[:])
 
         def bias_tensor(i, j):
             if j == 0:
@@ -284,7 +283,7 @@ def tile_transformerblock_pb_t_kernel(tc, x, ao, wo, bo, g2, w1, w3, out_0, out_
 
         transposes_a(0)
         copy_a(0)
-        bo_ps = psum.tile([P, D], F32, tag="bo_ps", bufs=1)
+        bo_ps = psum.tile([P, D], F32, tag="acc1")
         nc.tensor.matmul(out=bo_ps[:], lhsT=ones[:], rhs=vecs[:, 0, :], start=True, stop=True)
         bo_all = consts.tile([P, D], BF16)
         nc.vector.tensor_copy(out=bo_all[:], in_=bo_ps[:])
@@ -314,9 +313,9 @@ def tile_transformerblock_pb_t_kernel(tc, x, ao, wo, bo, g2, w1, w3, out_0, out_
             quantise(k)
             run(product, k - 3)
             if k == -2:
-                bias_vector(1)
+                bias_share(1)
             if k >= 0:
-                run(bias_vector, k + 2)
+                run(bias_share, k + 2)
             run(gate_matmuls, k - 2)
             if k == 0:
                 lay_out_gate_weights()

from contextlib import ExitStack

import concourse.mybir as mybir
from concourse.masks import make_identity

BF16 = mybir.dt.bfloat16
F32 = mybir.dt.float32
U32 = mybir.dt.uint32
U8 = mybir.dt.uint8
FP8X4 = mybir.dt.float8_e4m3fn_x4
ALU = mybir.AluOpType
ACT = mybir.ActivationFunctionType

B, S, D, H, DK, F = 2, 2048, 512, 4, 128, 256
EPS = 1e-6
P = 128
PACK = 4
T_PER_P = S // P
PAIR = 2
N_PAIRS = B * T_PER_P // PAIR
HEAD_PAIRS = 1
WO_VECTOR = 320
D_GPSIMD = 464
FLOPS = 2 * B * S * (H * DK * D + D * 2 * F)


def tile_transformerblock_pb_t_kernel(tc, x, ao, wo, bo, g2, w1, w3, out_0, out_1):
    nc = tc.nc
    x_view = x.rearrange("b (p t) d -> b p t d", t=T_PER_P)
    ao_view = ao.rearrange("b h (p t) d -> b p h t d", t=T_PER_P)
    x1_view = out_0.rearrange("b (p t) d -> b p t d", t=T_PER_P)
    h_view = out_1.rearrange("b (p t) f -> b p t f", t=T_PER_P)

    with ExitStack() as ctx:
        ctx.enter_context(tc.manual_schedule())
        consts = ctx.enter_context(tc.tile_pool(name="consts", bufs=1))
        loads = ctx.enter_context(tc.tile_pool(name="loads", bufs=N_PAIRS))
        work = ctx.enter_context(tc.tile_pool(name="work", bufs=3))
        outs = ctx.enter_context(tc.tile_pool(name="outs", bufs=10))
        psum = ctx.enter_context(tc.psum_pool(name="psum", bufs=2))

        vecs = consts.tile([P, 2, D], BF16)
        nc.vector.memset(vecs[:], 0.0)

        wo_raw = consts.tile([P, PACK, D], BF16)
        w1_raw = consts.tile([P, PACK, F], BF16)
        w3_raw = consts.tile([P, PACK, F], BF16)
        nc.sync.dma_start(
            out=wo_raw[:].rearrange("p (u e) n -> p u (e n)", u=2),
            in_=wo.rearrange("(u p e) n -> p u (e n)", u=2, e=2),
        )
        a_sb = []
        x_sb = []
        for i in range(N_PAIRS):
            b, t0 = i // (N_PAIRS // B), (i % (N_PAIRS // B)) * PAIR
            a_pair = loads.tile([P, PAIR, H, DK], BF16, name="a_pair", tag="a_pair")
            for j in range(PAIR):
                nc.sync.dma_start(out=a_pair[:, j, :, :], in_=ao_view[b, :, :, t0 + j, :])
            if i == 0:
                nc.sync.dma_start(out=vecs[0:1, 0, :], in_=bo.unsqueeze(0))
                nc.sync.dma_start(out=vecs[0:1, 1, :], in_=g2.unsqueeze(0))
            x_pair = loads.tile([P, PAIR, D], BF16, name="x_pair", tag="x_pair")
            nc.sync.dma_start(out=x_pair[:], in_=x_view[b, :, t0 : t0 + PAIR, :])
            a_sb.append(a_pair)
            x_sb.append(x_pair)
            if i == 2:
                nc.sync.dma_start(
                    out=w1_raw[:].rearrange("p (u e) f -> p u (e f)", u=2),
                    in_=w1.rearrange("(u p e) f -> p u (e f)", u=2, e=2),
                )
                nc.sync.dma_start(
                    out=w3_raw[:].rearrange("p (u e) f -> p u (e f)", u=2),
                    in_=w3.rearrange("(u p e) f -> p u (e f)", u=2, e=2),
                )

        warm = consts.tile([P, 2], F32)
        nc.vector.memset(warm[:], 0.0)
        nc.scalar.activation(out=warm[:, 1:2], in_=warm[:, 0:1], func=ACT.Silu)
        ident_f32 = consts.tile([P, P], F32)
        make_identity(nc, ident_f32[:])
        ident_bf16 = consts.tile([P, P], BF16)
        make_identity(nc, ident_bf16[:])
        ones = consts.tile([P, P], BF16)
        nc.vector.memset(ones[:], 1.0)
        neg_half = consts.tile([P, PAIR], F32)
        nc.vector.memset(neg_half[:], -0.5)
        eps = consts.tile([P, 1], F32)
        nc.vector.memset(eps[:], EPS)

        wo_grp = consts.tile([P, D, PACK], BF16, align_bytes=64)
        wo_codes = consts.tile([P, D], U32, align_bytes=64)
        wo_scales = consts.tile([P, D], U8, align_bytes=64)
        nc.vector.tensor_copy(out=wo_grp[:, 0:WO_VECTOR, :], in_=wo_raw[:, :, 0:WO_VECTOR].rearrange("p j n -> p n j"))
        nc.scalar.copy(out=wo_grp[:, WO_VECTOR:D, :], in_=wo_raw[:, :, WO_VECTOR:D].rearrange("p j n -> p n j"))
        nc.vector.quantize_mx(
            out=wo_codes[:].bitcast(FP8X4),
            scales=wo_scales[:],
            in_=wo_grp[:].rearrange("p n j -> p (n j)"),
        )
        w13_grp = consts.tile([P, 2 * F, PACK], BF16, align_bytes=64)
        w13_codes = consts.tile([P, 2 * F], U32, align_bytes=64)
        w13_scales = consts.tile([P, 2 * F], U8, align_bytes=64)

        def lay_out_gate_weights():
            nc.vector.tensor_copy(out=w13_grp[:, 0:F, :], in_=w1_raw[:].rearrange("p j f -> p f j"))
            nc.vector.tensor_copy(out=w13_grp[:, F : 2 * F, :], in_=w3_raw[:].rearrange("p j f -> p f j"))

        def quantise_gate_weights():
            nc.vector.quantize_mx(
                out=w13_codes[:].bitcast(FP8X4),
                scales=w13_scales[:],
                in_=w13_grp[:].rearrange("p n j -> p (n j)"),
            )

        live = {}

        def group_tile(k):
            if ("grp", k) not in live:
                grp = work.tile([P, 2, PAIR * P, 2], F32, align_bytes=64)
                live["grp", k] = grp
            return live["grp", k]

        def transposes_a(i):
            a_t = psum.tile([P, 2, PAIR * P], F32, tag="a_t", bufs=1)
            for j in range(PAIR):
                a_words = a_sb[i][:, j, :, :].rearrange("p h d -> p (h d)").bitcast(F32)
                for u in range(2):
                    nc.tensor.transpose(
                        a_t[:, u, j * P : (j + 1) * P], a_words[:, u * P : (u + 1) * P], ident_f32[:]
                    )
            live["a_t", i] = a_t

        def copy_a(i):
            nc.scalar.copy(out=group_tile(i - 2)[:, 0, :, :], in_=live["a_t", i][:].rearrange("p u t -> p t u"))

        def bias_gpsimd(i):
            xb = work.tile([P, PAIR, D], F32, bufs=4)
            nc.gpsimd.tensor_tensor(
                out=xb[:, :, 0:D_GPSIMD],
                in0=x_sb[i][:, :, 0:D_GPSIMD],
                in1=bo_all[:, 0:D_GPSIMD].unsqueeze(1).to_broadcast([P, PAIR, D_GPSIMD]),
                op=ALU.add,
            )
            live["xb", i] = xb

        def bias_share(i):
            part_ps = psum.tile([P, PAIR, D - D_GPSIMD], F32, tag="part_ps", bufs=1)
            for j in range(PAIR):
                nc.tensor.matmul(out=part_ps[:, j, :], lhsT=ident_bf16[:], rhs=x_sb[i][:, j, D_GPSIMD:D], start=True, stop=False)
                nc.tensor.matmul(out=part_ps[:, j, :], lhsT=ones[:], rhs=vecs[:, 0, D_GPSIMD:D], start=False, stop=True)
            nc.scalar.copy(out=live["xb", i][:, :, D_GPSIMD:D], in_=part_ps[:])

        def bias_tensor(i, j):
            if j == 0:
                xb = work.tile([P, PAIR, D], F32, bufs=4)
                live["xb", i] = xb
            xb_ps = psum.tile([P, D], F32, name="xb_ps", tag=("u_ps", "v_ps")[j], bufs=1)
            nc.tensor.matmul(out=xb_ps[:], lhsT=ident_bf16[:], rhs=x_sb[i][:, j, :], start=True, stop=False)
            nc.tensor.matmul(out=xb_ps[:], lhsT=ones[:], rhs=vecs[:, 0, :], start=False, stop=True)
            nc.scalar.copy(out=live["xb", i][:, j, :], in_=xb_ps[:])

        def quantise(k):
            first = 0 if 0 <= k + 2 < N_PAIRS else 1
            last = 2 if 0 <= k - 2 < N_PAIRS else 1
            if first >= last:
                return
            codes = work.tile([P, 2, PAIR * P], U32, align_bytes=64)
            scales = work.tile([P, 2, PAIR * P], U8, align_bytes=64)
            nc.vector.quantize_mx(
                out=codes[:, first:last, :].rearrange("p s t -> p (s t)").bitcast(FP8X4),
                scales=scales[:, first:last, :].rearrange("p s t -> p (s t)"),
                in_=group_tile(k)[:, first:last, :, :].rearrange("p s t u -> p (s t u)").bitcast(BF16),
            )
            live["codes", k] = codes
            live["scales", k] = scales

        def project(i, j):
            cols = slice(j * P, (j + 1) * P)
            acc1 = psum.tile([P, D], F32, tag="acc1")
            nc.tensor.matmul_mx(
                out=acc1[:],
                lhsT=live["codes", i - 2][:, 0, cols].bitcast(FP8X4),
                lhsT_scale=live["scales", i - 2][:, 0, cols],
                rhs=wo_codes[:].bitcast(FP8X4),
                rhs_scale=wo_scales[:],
                start=True,
                stop=True,
            )
            live["acc1", i, j] = acc1

        def residual(i, j):
            if j == 0:
                x1 = outs.tile([P, PAIR, D], F32)
                live["x1", i] = x1
            nc.vector.tensor_tensor(
                out=live["x1", i][:, j, :], in0=live["acc1", i, j][:], in1=live["xb", i][:, j, :], op=ALU.add
            )

        def store_x1(i):
            b, t0 = i // (N_PAIRS // B), (i % (N_PAIRS // B)) * PAIR
            nc.sync.dma_start(out=x1_view[b, :, t0 : t0 + PAIR, :], in_=live["x1", i][:])

        def squares(i, j):
            if j == 0:
                ssq = work.tile([P, PAIR], F32)
                live["ssq", i] = ssq
            unread = work.tile([P, D], BF16, bufs=4)
            nc.scalar.activation(
                out=unread[:],
                in_=live["x1", i][:, j, :],
                func=ACT.Square,
                accum_out=live["ssq", i][:, j : j + 1],
            )

        def mean_square(i):
            ms = work.tile([P, PAIR], F32)
            nc.scalar.activation(out=ms[:], in_=live["ssq", i][:], func=ACT.Identity, scale=1.0 / D, bias=eps[:])
            live["ms", i] = ms

        def rsqrt(i):
            r = work.tile([P, PAIR], F32)
            nc.gpsimd.tensor_tensor(out=r[:], in0=live["ms", i][:], in1=neg_half[:], op=ALU.pow)
            live["r", i] = r

        def normalise(i):
            n_sb = work.tile([P, PAIR, D], BF16)
            for j in range(PAIR):
                nc.vector.scalar_tensor_tensor(
                    out=n_sb[:, j, :],
                    in0=live["x1", i][:, j, :],
                    scalar=live["r", i][:, j : j + 1],
                    in1=g2_ps[:],
                    op0=ALU.mult,
                    op1=ALU.mult,
                )
            live["n_sb", i] = n_sb

        def transposes_n(i):
            n_t = psum.tile([P, 2, PAIR * P], F32, tag="n_t", bufs=1)
            for j in range(PAIR):
                n_words = live["n_sb", i][:, j, :].bitcast(F32)
                for u in range(2):
                    nc.tensor.transpose(
                        n_t[:, u, j * P : (j + 1) * P], n_words[:, u * P : (u + 1) * P], ident_f32[:]
                    )
            live["n_t", i] = n_t

        def copy_n(i):
            nc.scalar.copy(out=group_tile(i + 2)[:, 1, :, :], in_=live["n_t", i][:].rearrange("p u t -> p t u"))

        def gate_matmuls(i):
            u_ps = psum.tile([P, PAIR, F], F32, tag="u_ps", bufs=1)
            v_ps = psum.tile([P, PAIR, F], F32, tag="v_ps", bufs=1)
            for out_ps, w_cols in ((u_ps, slice(0, F)), (v_ps, slice(F, 2 * F))):
                for j in range(PAIR):
                    cols = slice(j * P, (j + 1) * P)
                    nc.tensor.matmul_mx(
                        out=out_ps[:, j, :],
                        lhsT=live["codes", i + 2][:, 1, cols].bitcast(FP8X4),
                        lhsT_scale=live["scales", i + 2][:, 1, cols],
                        rhs=w13_codes[:, w_cols].bitcast(FP8X4),
                        rhs_scale=w13_scales[:, w_cols],
                        start=True,
                        stop=True,
                    )
            live["u_ps", i] = u_ps
            live["v_ps", i] = v_ps

        def silu(i):
            gate = work.tile([P, PAIR, F], F32)
            nc.scalar.activation(out=gate[:], in_=live["u_ps", i][:], func=ACT.Silu)
            live["gate", i] = gate

        def product(i):
            h_sb = outs.tile([P, PAIR, F], F32)
            nc.vector.tensor_tensor(out=h_sb[:], in0=live["v_ps", i][:], in1=live["gate", i][:], op=ALU.mult)
            b, t0 = i // (N_PAIRS // B), (i % (N_PAIRS // B)) * PAIR
            nc.sync.dma_start(out=h_view[b, :, t0 : t0 + PAIR, :], in_=h_sb[:])

        def run(stage, i, *tile):
            if 0 <= i < N_PAIRS:
                stage(i, *tile)

        transposes_a(0)
        copy_a(0)
        bo_ps = psum.tile([P, D], F32, tag="acc1")
        nc.tensor.matmul(out=bo_ps[:], lhsT=ones[:], rhs=vecs[:, 0, :], start=True, stop=True)
        bo_all = consts.tile([P, D], BF16)
        nc.vector.tensor_copy(out=bo_all[:], in_=bo_ps[:])
        g2_ps = psum.tile([P, D], F32, tag="g2_ps", bufs=1)
        nc.tensor.matmul(out=g2_ps[:], lhsT=ones[:], rhs=vecs[:, 1, :], start=True, stop=True)
        bias_tensor(0, 0)
        bias_gpsimd(1)
        for k in range(-2, N_PAIRS + 3):
            for j in range(PAIR):
                run(residual, k, j)
                run(project, k + 1, j)
            run(store_x1, k)
            run(silu, k - 3)
            run(squares, k, 0)
            run(squares, k, 1)
            run(mean_square, k)
            run(rsqrt, k)
            if k >= 0:
                run(bias_gpsimd, k + 2)
            run(normalise, k - 1)
            run(transposes_a, k + 3)
            run(copy_a, k + 3)
            if k == -2:
                bias_tensor(0, 1)
            run(transposes_n, k - 1)
            run(copy_n, k - 1)
            quantise(k)
            run(product, k - 3)
            if k == -2:
                bias_share(1)
            if k >= 0:
                run(bias_share, k + 2)
            run(gate_matmuls, k - 2)
            if k == 0:
                lay_out_gate_weights()
                quantise_gate_weights()
